import numpy as np
import ml_dtypes


def mxq(x, axis, fmt="e4m3"):
    dtype, down = {"e4m3": (ml_dtypes.float8_e4m3fn, 7), "e5m2": (ml_dtypes.float8_e5m2, 14)}[fmt]
    v = np.moveaxis(np.asarray(x, np.float32).astype(ml_dtypes.bfloat16).astype(np.float64), axis, -1)
    blocks = v.reshape(v.shape[:-1] + (-1, 32))
    amax = np.abs(blocks).max(-1, keepdims=True)
    byte = np.maximum(np.where(amax > 0, np.frexp(amax)[1] - 1 + 127, 0) - down, 1)
    scale = np.exp2(byte - 127.0)
    codes = (blocks / scale).astype(np.float32).astype(dtype).astype(np.float64)
    return np.moveaxis((codes * scale).reshape(v.shape), -1, axis)


WIDE = False


def mx_kscale(k):
    if not WIDE:
        return np.ones(k)
    levels = np.array([10, -10, 5, -5, 0])
    if k % 512:
        return np.exp2(np.random.permutation(np.resize(levels, k // 32))).repeat(32)
    a = np.empty((k // 512, 16))
    for p in range(k // 512):
        a[p, :8] = np.random.permutation(np.resize(levels, 8))
        for g in range(8):
            far = levels[np.abs(levels - a[p, g]) >= 10]
            a[p, g + 8] = far[np.random.randint(len(far))]
    return np.exp2(a.ravel()).repeat(32)


BF16 = ml_dtypes.bfloat16


def bf(x):
    return np.asarray(x, np.float32).astype(BF16)


def f64(x):
    return np.asarray(x).astype(np.float64)


B, S, E, N_HEAD, MP_NUM, ROTARY_DIM = 2, 2048, 512, 4, 4, 64
HEAD_DIM = E // N_HEAD
LOCAL = E // MP_NUM
ROPE_BASE = 10000.0


def rotate_every_two(x):
    x1 = x[..., 0::2]
    x2 = x[..., 1::2]
    return np.stack((-x2, x1), axis=-1).reshape(x.shape)


def rope(x, sin, cos):
    x_rot = x[..., :ROTARY_DIM]
    x_pass = x[..., ROTARY_DIM:]
    x_rot = x_rot * cos + rotate_every_two(x_rot) * sin
    return np.concatenate([x_rot, x_pass], axis=-1)


def setup_inputs():
    s = mx_kscale(E)
    return {"hidden_states": bf(np.random.standard_normal((B, S, E)) * s),
            "w_qkv": bf(np.random.standard_normal((3 * E, E)) / np.sqrt(E) / s[None, :])}


def reference(hidden_states, w_qkv):
    qkv = mxq(f64(hidden_states), 2, "e4m3") @ mxq(f64(w_qkv), 1, "e4m3").T
    qkv = qkv.reshape(B, S, MP_NUM, 3 * LOCAL)
    q = qkv[..., :LOCAL].reshape(B, S, N_HEAD, HEAD_DIM)
    v = qkv[..., LOCAL:2 * LOCAL].reshape(B, S, N_HEAD, HEAD_DIM)
    k = qkv[..., 2 * LOCAL:].reshape(B, S, N_HEAD, HEAD_DIM)
    inv_freq = 1.0 / (ROPE_BASE ** (np.arange(0, ROTARY_DIM, 2) / ROTARY_DIM))
    freqs = np.arange(S)[:, None] * inv_freq[None, :]
    sin = np.repeat(np.sin(freqs), 2, axis=-1)[None, :, None, :]
    cos = np.repeat(np.cos(freqs), 2, axis=-1)[None, :, None, :]
    q = rope(q, sin, cos)
    k = rope(k, sin, cos)
    return q.transpose(0, 2, 1, 3), k.transpose(0, 2, 1, 3), v.transpose(0, 2, 1, 3)

@@ -1,0 +1,247 @@
+import math
+from contextlib import ExitStack
+
+import concourse.mybir as mybir
+from concourse.masks import make_identity
+
+F32 = mybir.dt.float32
+BF16 = mybir.dt.bfloat16
+I32 = mybir.dt.int32
+U32 = mybir.dt.uint32
+U8 = mybir.dt.uint8
+FP8X4 = mybir.dt.float8_e4m3fn_x4
+ALU = mybir.AluOpType
+ACT = mybir.ActivationFunctionType
+
+P = 128
+BATCH, SEQ, CHANNELS = 2, 2048, 512
+HEADS, HEAD_DIM, ROTARY = 4, 128, 64
+PAIRS = ROTARY // 2
+ROPE_BASE = 10000.0
+QUERY, VALUE, KEY = 0, 1, 2
+TILES = SEQ // P
+BANK = 512
+ROTARY_BANK, PLAIN_BANK, VALUE_BANK = 0, 1, 2
+CHUNK = 4
+STAGE = 8
+ROUND_MAGIC = 12582912.0
+COARSE_STEP = 2.0**-15
+SPLIT_PAIRS = 12
+VECTOR_ADDS_EVERY = 4
+
+FLOPS = 2 * BATCH * SEQ * CHANNELS * 3 * CHANNELS
+
+
+def reduced_angles(nc, pool):
+    position_int = pool.tile([P, TILES], I32)
+    nc.gpsimd.iota(position_int[:], pattern=[[1, TILES]], base=0, channel_multiplier=TILES)
+    position = pool.tile([P, TILES], F32)
+    nc.vector.tensor_copy(out=position[:], in_=position_int[:])
+
+    turns = pool.tile([P, PAIRS, TILES], F32)
+    rest = pool.tile([P, SPLIT_PAIRS, TILES], F32)
+    for i in range(PAIRS):
+        frequency = ROPE_BASE ** (-i / PAIRS) / (2.0 * math.pi)
+        if i < SPLIT_PAIRS:
+            coarse = round(frequency / COARSE_STEP) * COARSE_STEP
+            nc.vector.tensor_scalar_mul(out=turns[:, i, :], in0=position[:], scalar1=coarse)
+            nc.scalar.mul(out=rest[:, i, :], in_=position[:], mul=frequency - coarse)
+        else:
+            nc.vector.tensor_scalar_mul(out=turns[:, i, :], in0=position[:], scalar1=frequency)
+
+    whole = pool.tile([P, PAIRS, TILES], F32)
+
+    def drop_whole_turns():
+        nc.vector.tensor_scalar(
+            out=whole[:], in0=turns[:], scalar1=ROUND_MAGIC, scalar2=ROUND_MAGIC, op0=ALU.add, op1=ALU.subtract
+        )
+        nc.vector.tensor_sub(out=turns[:], in0=turns[:], in1=whole[:])
+
+    drop_whole_turns()
+    nc.vector.tensor_add(out=turns[:, :SPLIT_PAIRS, :], in0=turns[:, :SPLIT_PAIRS, :], in1=rest[:])
+    drop_whole_turns()
+
+    quarter = pool.tile([P, PAIRS, TILES], F32)
+    nc.vector.scalar_tensor_tensor(
+        out=quarter[:], in0=turns[:], scalar=-1.0, in1=turns[:], op0=ALU.mult, op1=ALU.min
+    )
+    nc.vector.tensor_scalar_add(out=quarter[:], in0=quarter[:], scalar1=0.25)
+    return turns, quarter
+
+
+def sine_table(nc, pool, turns, name):
+    table = pool.tile([P, TILES, PAIRS], F32, name=name)
+    nc.scalar.activation(out=table[:], in_=turns[:].rearrange("p i t -> p t i"), func=ACT.Sin, scale=2.0 * math.pi)
+    return table
+
+
+def tile_ttcodegenattention_pa_t_kernel(tc, hidden_states, w_qkv, out_0, out_1, out_2):
+    nc = tc.nc
+    chunks_in_batch = TILES // CHUNK
+
+    with ExitStack() as ctx:
+        const = ctx.enter_context(tc.tile_pool(name="const", bufs=1))
+        tokens_in = ctx.enter_context(tc.tile_pool(name="tokens_in", bufs=BATCH * chunks_in_batch))
+        tokens_grouped = ctx.enter_context(tc.tile_pool(name="tokens_grouped", bufs=2))
+        tokens_mx = ctx.enter_context(tc.tile_pool(name="tokens_mx", bufs=3))
+        products = ctx.enter_context(tc.tile_pool(name="products", bufs=3))
+        stage = ctx.enter_context(tc.tile_pool(name="stage", bufs=2))
+        turned_psum = ctx.enter_context(tc.psum_pool(name="turned_psum", bufs=2))
+        result_psum = ctx.enter_context(tc.psum_pool(name="result_psum", bufs=2))
+
+        identity = const.tile([P, P], F32)
+        make_identity(nc, identity[:])
+
+        warm = const.tile([P, 1], F32)
+        nc.vector.memset(warm[:], 0.0)
+        nc.scalar.activation(out=warm[:], in_=warm[:], func=ACT.Sin)
+
+        weights_in = const.tile([P, 3, HEADS, CHANNELS], BF16)
+        weights_by_kind = w_qkv.rearrange("(s c p) k -> c p s k", c=3, p=P)
+        tokens_by_partition = hidden_states.rearrange("b (p t) k -> b p t k", t=TILES)
+        chunk_list = [(b, c) for b in range(BATCH) for c in range(chunks_in_batch)]
+        raw_tokens = {}
+
+        def load_weights(kind):
+            nc.sync.dma_start(out=weights_in[:, kind, :, :], in_=weights_by_kind[kind])
+
+        def load_tokens(b, c):
+            raw = tokens_in.tile([P, CHUNK, CHANNELS], BF16, name="raw")
+            nc.sync.dma_start(out=raw[:], in_=tokens_by_partition[b][:, c * CHUNK : (c + 1) * CHUNK, :])
+            raw_tokens[(b, c)] = raw
+
+        load_weights(QUERY)
+        load_weights(KEY)
+        load_tokens(0, 0)
+        load_weights(VALUE)
+        for b, c in chunk_list[1:]:
+            load_tokens(b, c)
+
+        sine_turns, cosine_turns = reduced_angles(nc, const)
+
+        def turn_two_rows_blocks(first, second):
+            turned = turned_psum.tile([P, 2, 2, P], F32, name="turned")
+            for a, block in enumerate((first, second)):
+                words = block.bitcast(F32)
+                for u in range(2):
+                    nc.tensor.transpose(out=turned[:, a, u, :], in_=words[:, u::2], identity=identity[:])
+            return turned
+
+        weights_grouped = const.tile([P, 3, BANK, 4], BF16, align_bytes=64)
+        weights_codes = const.tile([P, 3, BANK], U32, align_bytes=64)
+        weights_scales = const.tile([P, 3, BANK], U8, align_bytes=64)
+        grouped_words = weights_grouped[:].bitcast(F32)
+
+        def quantise_weights(bank):
+            nc.vector.quantize_mx(
+                out=weights_codes[:, bank, :].bitcast(FP8X4),
+                scales=weights_scales[:, bank, :],
+                in_=weights_grouped[:, bank, :, :].rearrange("p n v -> p (n v)"),
+            )
+
+        for slot, kind in ((0, QUERY), (HEADS, KEY)):
+            for h in range(0, HEADS, 2):
+                turned = turn_two_rows_blocks(weights_in[:, kind, h, :], weights_in[:, kind, h + 1, :])
+                for a in range(2):
+                    g = slot + h + a
+                    nc.scalar.copy(
+                        out=grouped_words[:, ROTARY_BANK : PLAIN_BANK + 1, g * ROTARY : (g + 1) * ROTARY, :],
+                        in_=turned[:, a, :, :].rearrange("p u (r d) -> p r d u", r=2),
+                    )
+        quantise_weights(ROTARY_BANK)
+        quantise_weights(PLAIN_BANK)
+
+        def quantise_tokens(b, c):
+            raw = raw_tokens[(b, c)]
+            grouped = tokens_grouped.tile([P, CHUNK, P, 4], BF16, align_bytes=64, name="grouped")
+            for a in range(0, CHUNK, 2):
+                turned = turn_two_rows_blocks(raw[:, a, :], raw[:, a + 1, :])
+                nc.scalar.copy(
+                    out=grouped[:, a : a + 2, :, :].bitcast(F32),
+                    in_=turned[:].rearrange("p a u r -> p a r u"),
+                )
+            codes = tokens_mx.tile([P, CHUNK, P], U32, align_bytes=64, name="codes")
+            scales = tokens_mx.tile([P, CHUNK, P], U8, align_bytes=64, name="scales")
+            nc.vector.quantize_mx(
+                out=codes[:].rearrange("p a r -> p (a r)").bitcast(FP8X4),
+                scales=scales[:].rearrange("p a r -> p (a r)"),
+                in_=grouped[:].rearrange("p a r v -> p (a r v)"),
+            )
+            return codes, scales
+
+        def project(codes, scales, a, bank, name):
+            result = result_psum.tile([P, BANK], F32, name=name)
+            nc.tensor.matmul_mx(
+                out=result[:],
+                lhsT=codes[:, a, :].bitcast(FP8X4),
+                lhsT_scale=scales[:, a, :],
+                rhs=weights_codes[:, bank, :].bitcast(FP8X4),
+                rhs_scale=weights_scales[:, bank, :],
+                start=True,
+                stop=True,
+            )
+            return result
+
+        out_views = [o.rearrange("b h (p t) d -> b p h t d", t=TILES) for o in (out_0, out_1, out_2)]
+
+        ready = quantise_tokens(*chunk_list[0])
+
+        for h in range(0, HEADS, 2):
+            turned = turn_two_rows_blocks(weights_in[:, VALUE, h, :], weights_in[:, VALUE, h + 1, :])
+            nc.scalar.copy(
+                out=grouped_words[:, VALUE_BANK, h * HEAD_DIM : (h + 2) * HEAD_DIM, :].rearrange(
+                    "p (a d) u -> p a d u", a=2
+                ),
+                in_=turned[:].rearrange("p a u d -> p a d u"),
+            )
+        quantise_weights(VALUE_BANK)
+
+        sin = sine_table(nc, const, sine_turns, "sin")
+        cos = sine_table(nc, const, cosine_turns, "cos")
+
+        for n, (b, c) in enumerate(chunk_list):
+            codes, scales = ready
+            if n + 1 < len(chunk_list):
+                ready = quantise_tokens(*chunk_list[n + 1])
+            if (c * CHUNK) % STAGE == 0:
+                stage_qk = stage.tile([P, 2 * HEADS, STAGE, HEAD_DIM], F32, name="stage_qk")
+                stage_v = stage.tile([P, HEADS, STAGE, HEAD_DIM], F32, name="stage_v")
+            for a in range(CHUNK):
+                t = c * CHUNK + a
+                place = t % STAGE
+
+                rotary = project(codes, scales, a, ROTARY_BANK, "rotary")
+                by_pair = rotary[:].rearrange("p (g i e) -> p g i e", g=2 * HEADS, e=2)
+                sin_t = sin[:, t, :].unsqueeze(1).to_broadcast([P, 2 * HEADS, PAIRS])
+                cos_t = cos[:, t, :].unsqueeze(1).unsqueeze(3).to_broadcast([P, 2 * HEADS, PAIRS, 2])
+                with_cos = products.tile([P, 2 * HEADS, PAIRS, 2], F32, name="with_cos")
+                with_sin = products.tile([P, 2, 2 * HEADS, PAIRS], F32, name="with_sin")
+                nc.vector.tensor_tensor(out=with_cos[:], in0=by_pair, in1=cos_t, op=ALU.mult)
+                nc.vector.scalar_tensor_tensor(
+                    out=with_sin[:, 0, :, :], in0=by_pair[:, :, :, 1], scalar=-1.0, in1=sin_t, op0=ALU.mult, op1=ALU.mult
+                )
+                nc.vector.tensor_tensor(out=with_sin[:, 1, :, :], in0=by_pair[:, :, :, 0], in1=sin_t, op=ALU.mult)
+                adder = nc.vector if t % VECTOR_ADDS_EVERY == 0 else nc.gpsimd
+                adder.tensor_tensor(
+                    out=stage_qk[:, :, place, :ROTARY].rearrange("p g (i e) -> p g i e", e=2),
+                    in0=with_cos[:],
+                    in1=with_sin[:].rearrange("p e g i -> p g i e"),
+                    op=ALU.add,
+                )
+
+                plain = project(codes, scales, a, PLAIN_BANK, "plain")
+                nc.scalar.copy(
+                    out=stage_qk[:, :, place, ROTARY:], in_=plain[:].rearrange("p (g d) -> p g d", g=2 * HEADS)
+                )
+
+                value = project(codes, scales, a, VALUE_BANK, "value")
+                nc.scalar.copy(out=stage_v[:, :, place, :], in_=value[:].rearrange("p (h d) -> p h d", h=HEADS))
+
+            tiles_stored = STAGE // 2 if b == 0 else STAGE
+            done = (c + 1) * CHUNK
+            if done % tiles_stored == 0:
+                rows = slice(done - tiles_stored, done)
+                places = slice((done - tiles_stored) % STAGE, (done - 1) % STAGE + 1)
+                nc.sync.dma_start(out=out_views[2][b][:, :, rows, :], in_=stage_v[:, :, places, :])
+                nc.sync.dma_start(out=out_views[0][b][:, :, rows, :], in_=stage_qk[:, :HEADS, places, :])
+                nc.sync.dma_start(out=out_views[1][b][:, :, rows, :], in_=stage_qk[:, HEADS:, places, :])

@@ -18,77 +18,105 @@ BATCH, SEQ, CHANNELS = 2, 2048, 512
 HEADS, HEAD_DIM, ROTARY = 4, 128, 64
 PAIRS = ROTARY // 2
 ROPE_BASE = 10000.0
+VALUES_BESIDE = [0, 2, 2, 1, 1, 1, 1, 0, 0, 0, 1, 1, 1, 1]
+HALVES=16
+VH=0
+OUTPUT_OF = {0: 0, 1: 2, 2: 1}
 QUERY, VALUE, KEY = 0, 1, 2
 TILES = SEQ // P
-BANK = 512
-ROTARY_BANK, PLAIN_BANK, VALUE_BANK = 0, 1, 2
 CHUNK = 4
-STAGE = 8
+CHUNKS = TILES // CHUNK
 ROUND_MAGIC = 12582912.0
 COARSE_STEP = 2.0**-15
+DECADE = PAIRS // 4
+WHOLE_PAIRS = 23
 SPLIT_PAIRS = 12
-VECTOR_ADDS_EVERY = 4
 
 FLOPS = 2 * BATCH * SEQ * CHANNELS * 3 * CHANNELS
 
 
-def reduced_angles(nc, pool):
-    position_int = pool.tile([P, TILES], I32)
-    nc.gpsimd.iota(position_int[:], pattern=[[1, TILES]], base=0, channel_multiplier=TILES)
+def reduced_angles(nc, pool, position_int):
     position = pool.tile([P, TILES], F32)
     nc.vector.tensor_copy(out=position[:], in_=position_int[:])
 
-    turns = pool.tile([P, PAIRS, TILES], F32)
-    rest = pool.tile([P, SPLIT_PAIRS, TILES], F32)
+    turns = pool.tile([P, TILES, PAIRS], F32)
+    rest = pool.tile([P, TILES, SPLIT_PAIRS], F32)
     for i in range(PAIRS):
         frequency = ROPE_BASE ** (-i / PAIRS) / (2.0 * math.pi)
         if i < SPLIT_PAIRS:
             coarse = round(frequency / COARSE_STEP) * COARSE_STEP
-            nc.vector.tensor_scalar_mul(out=turns[:, i, :], in0=position[:], scalar1=coarse)
-            nc.scalar.mul(out=rest[:, i, :], in_=position[:], mul=frequency - coarse)
-        else:
-            nc.vector.tensor_scalar_mul(out=turns[:, i, :], in0=position[:], scalar1=frequency)
-
-    whole = pool.tile([P, PAIRS, TILES], F32)
-
-    def drop_whole_turns():
-        nc.vector.tensor_scalar(
-            out=whole[:], in0=turns[:], scalar1=ROUND_MAGIC, scalar2=ROUND_MAGIC, op0=ALU.add, op1=ALU.subtract
+            nc.vector.tensor_scalar_mul(out=turns[:, :, i], in0=position[:], scalar1=coarse)
+            nc.scalar.mul(out=rest[:, :, i], in_=position[:], mul=frequency - coarse)
+        elif i < SPLIT_PAIRS + DECADE:
+            nc.vector.tensor_scalar_mul(out=turns[:, :, i], in0=position[:], scalar1=frequency)
+    for i in range(SPLIT_PAIRS + DECADE, PAIRS, DECADE):
+        count = min(DECADE, PAIRS - i)
+        nc.vector.tensor_scalar_mul(
+            out=turns[:, :, i : i + count], in0=turns[:, :, i - DECADE : i - DECADE + count], scalar1=0.1
         )
-        nc.vector.tensor_sub(out=turns[:], in0=turns[:], in1=whole[:])
 
-    drop_whole_turns()
-    nc.vector.tensor_add(out=turns[:, :SPLIT_PAIRS, :], in0=turns[:, :SPLIT_PAIRS, :], in1=rest[:])
-    drop_whole_turns()
+    whole = pool.tile([P, TILES, PAIRS], F32)
 
-    quarter = pool.tile([P, PAIRS, TILES], F32)
-    nc.vector.scalar_tensor_tensor(
-        out=quarter[:], in0=turns[:], scalar=-1.0, in1=turns[:], op0=ALU.mult, op1=ALU.min
+    def drop_whole_turns(count):
+        nc.vector.tensor_scalar(
+            out=whole[:, :, :count],
+            in0=turns[:, :, :count],
+            scalar1=ROUND_MAGIC,
+            scalar2=ROUND_MAGIC,
+            op0=ALU.add,
+            op1=ALU.subtract,
+        )
+        nc.vector.tensor_sub(out=turns[:, :, :count], in0=turns[:, :, :count], in1=whole[:, :, :count])
+
+    drop_whole_turns(WHOLE_PAIRS)
+    nc.vector.tensor_add(out=turns[:, :, :SPLIT_PAIRS], in0=turns[:, :, :SPLIT_PAIRS], in1=rest[:])
+    drop_whole_turns(SPLIT_PAIRS)
+
+    return turns
+
+
+def rotation_factors(nc, pool, turns):
+    sign = pool.tile([P, 2], F32)
+    nc.gpsimd.memset(sign[:, 0:1], 1.0)
+    nc.gpsimd.memset(sign[:, 1:2], -1.0)
+    factors = pool.tile([P, TILES, 2, ROTARY], F32)
+    shape = [P, TILES, PAIRS, 2]
+    sine = pool.tile([P, TILES, PAIRS], F32)
+    half_sine = pool.tile([P, TILES, PAIRS], F32)
+    squared = pool.tile([P, TILES, PAIRS], F32)
+    nc.scalar.activation(out=half_sine[:], in_=turns[:], func=ACT.Sin, scale=math.pi)
+    nc.scalar.activation(out=sine[:], in_=turns[:], func=ACT.Sin, scale=2.0 * math.pi)
+    nc.gpsimd.tensor_tensor(out=squared[:], in0=half_sine[:], in1=half_sine[:], op=ALU.mult)
+    nc.gpsimd.tensor_scalar(
+        out=factors[:, :, 0, :].rearrange("p t (i e) -> p t i e", e=2),
+        in0=squared[:].unsqueeze(3).to_broadcast(shape),
+        scalar1=-2.0,
+        scalar2=1.0,
+        op0=ALU.mult,
+        op1=ALU.add,
     )
-    nc.vector.tensor_scalar_add(out=quarter[:], in0=quarter[:], scalar1=0.25)
-    return turns, quarter
-
-
-def sine_table(nc, pool, turns, name):
-    table = pool.tile([P, TILES, PAIRS], F32, name=name)
-    nc.scalar.activation(out=table[:], in_=turns[:].rearrange("p i t -> p t i"), func=ACT.Sin, scale=2.0 * math.pi)
-    return table
+    nc.gpsimd.tensor_tensor(
+        out=factors[:, :, 1, :].rearrange("p t (i e) -> p t i e", e=2),
+        in0=sine[:].unsqueeze(3).to_broadcast(shape),
+        in1=sign[:].unsqueeze(1).unsqueeze(1).to_broadcast(shape),
+        op=ALU.mult,
+    )
+    return factors
 
 
 def tile_ttcodegenattention_pa_t_kernel(tc, hidden_states, w_qkv, out_0, out_1, out_2):
     nc = tc.nc
-    chunks_in_batch = TILES // CHUNK
 
     with ExitStack() as ctx:
         const = ctx.enter_context(tc.tile_pool(name="const", bufs=1))
-        tokens_in = ctx.enter_context(tc.tile_pool(name="tokens_in", bufs=BATCH * chunks_in_batch))
-        tokens_grouped = ctx.enter_context(tc.tile_pool(name="tokens_grouped", bufs=2))
-        tokens_mx = ctx.enter_context(tc.tile_pool(name="tokens_mx", bufs=3))
-        products = ctx.enter_context(tc.tile_pool(name="products", bufs=3))
-        stage = ctx.enter_context(tc.tile_pool(name="stage", bufs=2))
-        turned_psum = ctx.enter_context(tc.psum_pool(name="turned_psum", bufs=2))
-        result_psum = ctx.enter_context(tc.psum_pool(name="result_psum", bufs=2))
+        tokens_grouped = ctx.enter_context(tc.tile_pool(name="tokens_grouped", bufs=3))
+        products_pool = ctx.enter_context(tc.tile_pool(name="products_pool", bufs=3))
+        stages = ctx.enter_context(tc.tile_pool(name="stages", bufs=6))
+        banks = ctx.enter_context(tc.psum_pool(name="banks_psum", bufs=8))
+        ctx.enter_context(tc.manual_schedule())
 
+        position_int = const.tile([P, TILES], I32)
+        nc.gpsimd.iota(position_int[:], pattern=[[1, TILES]], base=0, channel_multiplier=TILES)
         identity = const.tile([P, P], F32)
         make_identity(nc, identity[:])
 
@@ -99,149 +127,235 @@ def tile_ttcodegenattention_pa_t_kernel(tc, hidden_states, w_qkv, out_0, out_1, 
         weights_in = const.tile([P, 3, HEADS, CHANNELS], BF16)
         weights_by_kind = w_qkv.rearrange("(s c p) k -> c p s k", c=3, p=P)
         tokens_by_partition = hidden_states.rearrange("b (p t) k -> b p t k", t=TILES)
-        chunk_list = [(b, c) for b in range(BATCH) for c in range(chunks_in_batch)]
-        raw_tokens = {}
+        raw_tokens = [const.tile([P, TILES, CHANNELS], BF16, name="raw%d" % b) for b in range(BATCH)]
 
         def load_weights(kind):
             nc.sync.dma_start(out=weights_in[:, kind, :, :], in_=weights_by_kind[kind])
 
-        def load_tokens(b, c):
-            raw = tokens_in.tile([P, CHUNK, CHANNELS], BF16, name="raw")
-            nc.sync.dma_start(out=raw[:], in_=tokens_by_partition[b][:, c * CHUNK : (c + 1) * CHUNK, :])
-            raw_tokens[(b, c)] = raw
+        def load_tokens(b, first, count):
+            rows = slice(first, first + count)
+            nc.sync.dma_start(out=raw_tokens[b][:, rows, :], in_=tokens_by_partition[b][:, rows, :])
 
+        load_tokens(0, 0, CHUNK)
+        load_weights(VALUE)
+        for c in range(1, CHUNKS):
+            load_tokens(0, c * CHUNK, CHUNK)
         load_weights(QUERY)
         load_weights(KEY)
-        load_tokens(0, 0)
-        load_weights(VALUE)
-        for b, c in chunk_list[1:]:
-            load_tokens(b, c)
+        for half in range(2):
+            load_tokens(1, half * TILES // 2, TILES // 2)
 
-        sine_turns, cosine_turns = reduced_angles(nc, const)
+        turns = reduced_angles(nc, const, position_int)
 
-        def turn_two_rows_blocks(first, second):
-            turned = turned_psum.tile([P, 2, 2, P], F32, name="turned")
+        def turn_two_row_blocks(first, second):
+            turned = banks.tile([P, 2, 2, P], F32, name="bank")
             for a, block in enumerate((first, second)):
                 words = block.bitcast(F32)
                 for u in range(2):
                     nc.tensor.transpose(out=turned[:, a, u, :], in_=words[:, u::2], identity=identity[:])
             return turned
 
-        weights_grouped = const.tile([P, 3, BANK, 4], BF16, align_bytes=64)
-        weights_codes = const.tile([P, 3, BANK], U32, align_bytes=64)
-        weights_scales = const.tile([P, 3, BANK], U8, align_bytes=64)
-        grouped_words = weights_grouped[:].bitcast(F32)
+        copy_out = (nc.scalar.copy, nc.vector.tensor_copy)
 
-        def quantise_weights(bank):
-            nc.vector.quantize_mx(
-                out=weights_codes[:, bank, :].bitcast(FP8X4),
-                scales=weights_scales[:, bank, :],
-                in_=weights_grouped[:, bank, :, :].rearrange("p n v -> p (n v)"),
-            )
+        weights_grouped = const.tile([P, 3, HEADS * HEAD_DIM, 4], BF16, align_bytes=64)
+        weights_codes = const.tile([P, 3, HEADS * HEAD_DIM], U32, align_bytes=64)
+        weights_scales = const.tile([P, 3, HEADS * HEAD_DIM], U8, align_bytes=64)
 
-        for slot, kind in ((0, QUERY), (HEADS, KEY)):
-            for h in range(0, HEADS, 2):
-                turned = turn_two_rows_blocks(weights_in[:, kind, h, :], weights_in[:, kind, h + 1, :])
+        def turn_weights(kind, h):
+            return turn_two_row_blocks(weights_in[:, kind, h, :], weights_in[:, kind, h + 1, :])
+
+        def sort_weights(turned, kind, h, copy):
+            columns = weights_grouped[:, kind, h * HEAD_DIM : (h + 2) * HEAD_DIM, :].bitcast(F32)
+            if kind == VALUE:
+                copy(
+                    out=columns.rearrange("p (a d) u -> p a d u", a=2),
+                    in_=turned[:].rearrange("p a u d -> p a d u"),
+                )
+            else:
                 for a in range(2):
-                    g = slot + h + a
-                    nc.scalar.copy(
-                        out=grouped_words[:, ROTARY_BANK : PLAIN_BANK + 1, g * ROTARY : (g + 1) * ROTARY, :],
+                    copy(
+                        out=columns.rearrange("p (r a d) u -> p r a d u", r=2, a=2)[:, :, a, :, :],
                         in_=turned[:, a, :, :].rearrange("p u (r d) -> p r d u", r=2),
                     )
-        quantise_weights(ROTARY_BANK)
-        quantise_weights(PLAIN_BANK)
+
+        def quantise_weights(kind, first, heads):
+            columns = slice(first * HEAD_DIM, (first + heads) * HEAD_DIM)
+            nc.vector.quantize_mx(
+                out=weights_codes[:, kind, columns].bitcast(FP8X4),
+                scales=weights_scales[:, kind, columns],
+                in_=weights_grouped[:, kind, columns, :].rearrange("p n v -> p (n v)"),
+            )
+
+        token_codes = [const.tile([P, TILES, P], U32, align_bytes=64, name="codes%d" % b) for b in range(BATCH)]
+        token_scales = [const.tile([P, TILES, P], U8, align_bytes=64, name="scales%d" % b) for b in range(BATCH)]
+
+        grouped_tokens = {}
+
+        def turn_tokens(b, c):
+            tiles = range(c * CHUNK, (c + 1) * CHUNK, 2)
+            return [turn_two_row_blocks(raw_tokens[b][:, t, :], raw_tokens[b][:, t + 1, :]) for t in tiles]
+
+        def sort_tokens(turned, b, c, half, copy):
+            if half == 0:
+                grouped_tokens[(b, c)] = tokens_grouped.tile([P, CHUNK, P, 4], BF16, align_bytes=64, name="grouped")
+            copy(
+                out=grouped_tokens[(b, c)][:, 2 * half : 2 * half + 2, :, :].bitcast(F32),
+                in_=turned[half][:].rearrange("p a u r -> p a r u"),
+            )
 
         def quantise_tokens(b, c):
-            raw = raw_tokens[(b, c)]
-            grouped = tokens_grouped.tile([P, CHUNK, P, 4], BF16, align_bytes=64, name="grouped")
-            for a in range(0, CHUNK, 2):
-                turned = turn_two_rows_blocks(raw[:, a, :], raw[:, a + 1, :])
-                nc.scalar.copy(
-                    out=grouped[:, a : a + 2, :, :].bitcast(F32),
-                    in_=turned[:].rearrange("p a u r -> p a r u"),
-                )
-            codes = tokens_mx.tile([P, CHUNK, P], U32, align_bytes=64, name="codes")
-            scales = tokens_mx.tile([P, CHUNK, P], U8, align_bytes=64, name="scales")
+            rows = slice(c * CHUNK, (c + 1) * CHUNK)
             nc.vector.quantize_mx(
-                out=codes[:].rearrange("p a r -> p (a r)").bitcast(FP8X4),
-                scales=scales[:].rearrange("p a r -> p (a r)"),
-                in_=grouped[:].rearrange("p a r v -> p (a r v)"),
+                out=token_codes[b][:, rows, :].rearrange("p a r -> p (a r)").bitcast(FP8X4),
+                scales=token_scales[b][:, rows, :].rearrange("p a r -> p (a r)"),
+                in_=grouped_tokens[(b, c)][:].rearrange("p a r v -> p (a r v)"),
             )
-            return codes, scales
 
-        def project(codes, scales, a, bank, name):
-            result = result_psum.tile([P, BANK], F32, name=name)
-            nc.tensor.matmul_mx(
-                out=result[:],
-                lhsT=codes[:, a, :].bitcast(FP8X4),
-                lhsT_scale=scales[:, a, :],
-                rhs=weights_codes[:, bank, :].bitcast(FP8X4),
-                rhs_scale=weights_scales[:, bank, :],
-                start=True,
-                stop=True,
-            )
-            return result
-
-        out_views = [o.rearrange("b h (p t) d -> b p h t d", t=TILES) for o in (out_0, out_1, out_2)]
-
-        ready = quantise_tokens(*chunk_list[0])
-
-        for h in range(0, HEADS, 2):
-            turned = turn_two_rows_blocks(weights_in[:, VALUE, h, :], weights_in[:, VALUE, h + 1, :])
-            nc.scalar.copy(
-                out=grouped_words[:, VALUE_BANK, h * HEAD_DIM : (h + 2) * HEAD_DIM, :].rearrange(
-                    "p (a d) u -> p a d u", a=2
-                ),
-                in_=turned[:].rearrange("p a u d -> p a d u"),
-            )
-        quantise_weights(VALUE_BANK)
-
-        sin = sine_table(nc, const, sine_turns, "sin")
-        cos = sine_table(nc, const, cosine_turns, "cos")
-
-        for n, (b, c) in enumerate(chunk_list):
-            codes, scales = ready
-            if n + 1 < len(chunk_list):
-                ready = quantise_tokens(*chunk_list[n + 1])
-            if (c * CHUNK) % STAGE == 0:
-                stage_qk = stage.tile([P, 2 * HEADS, STAGE, HEAD_DIM], F32, name="stage_qk")
-                stage_v = stage.tile([P, HEADS, STAGE, HEAD_DIM], F32, name="stage_v")
+        def project(result, b, c, kind, group):
+            columns = slice(group * P, (group + 1) * P)
             for a in range(CHUNK):
                 t = c * CHUNK + a
-                place = t % STAGE
-
-                rotary = project(codes, scales, a, ROTARY_BANK, "rotary")
-                by_pair = rotary[:].rearrange("p (g i e) -> p g i e", g=2 * HEADS, e=2)
-                sin_t = sin[:, t, :].unsqueeze(1).to_broadcast([P, 2 * HEADS, PAIRS])
-                cos_t = cos[:, t, :].unsqueeze(1).unsqueeze(3).to_broadcast([P, 2 * HEADS, PAIRS, 2])
-                with_cos = products.tile([P, 2 * HEADS, PAIRS, 2], F32, name="with_cos")
-                with_sin = products.tile([P, 2, 2 * HEADS, PAIRS], F32, name="with_sin")
-                nc.vector.tensor_tensor(out=with_cos[:], in0=by_pair, in1=cos_t, op=ALU.mult)
-                nc.vector.scalar_tensor_tensor(
-                    out=with_sin[:, 0, :, :], in0=by_pair[:, :, :, 1], scalar=-1.0, in1=sin_t, op0=ALU.mult, op1=ALU.mult
-                )
-                nc.vector.tensor_tensor(out=with_sin[:, 1, :, :], in0=by_pair[:, :, :, 0], in1=sin_t, op=ALU.mult)
-                adder = nc.vector if t % VECTOR_ADDS_EVERY == 0 else nc.gpsimd
-                adder.tensor_tensor(
-                    out=stage_qk[:, :, place, :ROTARY].rearrange("p g (i e) -> p g i e", e=2),
-                    in0=with_cos[:],
-                    in1=with_sin[:].rearrange("p e g i -> p g i e"),
-                    op=ALU.add,
+                nc.tensor.matmul_mx(
+                    out=result[:, a, :],
+                    lhsT=token_codes[b][:, t, :].bitcast(FP8X4),
+                    lhsT_scale=token_scales[b][:, t, :],
+                    rhs=weights_codes[:, kind, columns].bitcast(FP8X4),
+                    rhs_scale=weights_scales[:, kind, columns],
+                    start=True,
+                    stop=True,
                 )
 
-                plain = project(codes, scales, a, PLAIN_BANK, "plain")
-                nc.scalar.copy(
-                    out=stage_qk[:, :, place, ROTARY:], in_=plain[:].rearrange("p (g d) -> p g d", g=2 * HEADS)
-                )
+        out_views = [o.rearrange("b h (p t) d -> b p h t d", t=TILES) for o in (out_0, out_1, out_2)]
+        staged = {}
 
-                value = project(codes, scales, a, VALUE_BANK, "value")
-                nc.scalar.copy(out=stage_v[:, :, place, :], in_=value[:].rearrange("p (h d) -> p h d", h=HEADS))
+        def stage_of(b, kind, h):
+            if (b, kind, h) not in staged:
+                staged[(b, kind, h)] = stages.tile([P, 2, TILES, HEAD_DIM], F32, name="stage")
+            return staged[(b, kind, h)]
 
-            tiles_stored = STAGE // 2 if b == 0 else STAGE
-            done = (c + 1) * CHUNK
-            if done % tiles_stored == 0:
-                rows = slice(done - tiles_stored, done)
-                places = slice((done - tiles_stored) % STAGE, (done - 1) % STAGE + 1)
-                nc.sync.dma_start(out=out_views[2][b][:, :, rows, :], in_=stage_v[:, :, places, :])
-                nc.sync.dma_start(out=out_views[0][b][:, :, rows, :], in_=stage_qk[:, :HEADS, places, :])
-                nc.sync.dma_start(out=out_views[1][b][:, :, rows, :], in_=stage_qk[:, HEADS:, places, :])
+        def store(b, kind, h, first, count):
+            rows = slice(first, first + count)
+            view = out_views[OUTPUT_OF[kind]][b]
+            nc.sync.dma_start(out=view[:, h : h + 2, rows, :], in_=stage_of(b, kind, h)[:, :, rows, :])
+
+        def value_unit(b, h, c, copy):
+            pair, head = h // 2 * 2, h % 2
+            value = banks.tile([P, CHUNK, P], F32, name="bank")
+            project(value, b, c, VALUE, h)
+            copy(out=stage_of(b, VALUE, pair)[:, head, c * CHUNK : (c + 1) * CHUNK, :], in_=value[:])
+
+        def project_rotary(b, kind, h, c):
+            rotary = banks.tile([P, CHUNK, P], F32, name="bank")
+            project(rotary, b, c, kind, h)
+            return rotary
+
+        def by_tile(b, kind, h, c):
+            return stage_of(b, kind, h)[:, :, c * CHUNK : (c + 1) * CHUNK, :].rearrange("p h t d -> p t h d")
+
+        def rotate(rotary, b, kind, h, c):
+            rows = slice(c * CHUNK, (c + 1) * CHUNK)
+            products = products_pool.tile([P, CHUNK, 2, P], F32, name="products")
+            shape = [P, CHUNK, 2, 2, ROTARY]
+            nc.vector.tensor_tensor(
+                out=products[:].rearrange("p t k (h d) -> p t k h d", h=2),
+                in0=rotary[:].rearrange("p t (h d) -> p t h d", h=2).unsqueeze(2).to_broadcast(shape),
+                in1=factors[:, rows, :, :].unsqueeze(3).to_broadcast(shape),
+                op=ALU.mult,
+            )
+            nc.gpsimd.tensor_tensor(
+                out=by_tile(b, kind, h, c)[:, :, :, :ROTARY].rearrange("p t h (i e) -> p t h i e", e=2),
+                in0=products[:, :, 0, :].rearrange("p t (h i e) -> p t h i e", h=2, e=2),
+                in1=products[:, :, 1, :].rearrange("p t (h i e) -> p t h i e", h=2, e=2)[:, :, :, :, ::-1],
+                op=ALU.add,
+            )
+
+        def plain_unit(b, kind, h, c):
+            plain = banks.tile([P, CHUNK, P], F32, name="bank")
+            project(plain, b, c, kind, h + 1)
+            nc.scalar.copy(
+                out=by_tile(b, kind, h, c)[:, :, :, ROTARY:], in_=plain[:].rearrange("p t (h d) -> p t h d", h=2)
+            )
+
+        scalar_copy, vector_copy = copy_out
+
+        turned = turn_tokens(0, 0)
+        sort_tokens(turned, 0, 0, 0, scalar_copy)
+        factors = rotation_factors(nc, const, turns)
+        sort_tokens(turned, 0, 0, 1, vector_copy)
+        turned_weights = [turn_weights(VALUE, 0), turn_weights(VALUE, 2)]
+        sort_weights(turned_weights[0], VALUE, 0, scalar_copy)
+        quantise_tokens(0, 0)
+        sort_weights(turned_weights[1], VALUE, 2, vector_copy)
+        turned = turn_tokens(0, 1)
+        sort_tokens(turned, 0, 1, 0, scalar_copy)
+        quantise_weights(VALUE, 0, HEADS)
+        sort_tokens(turned, 0, 1, 1, vector_copy)
+        turned = turn_tokens(0, 2)
+        sort_tokens(turned, 0, 2, 0, scalar_copy)
+        quantise_tokens(0, 1)
+        sort_tokens(turned, 0, 2, 1, vector_copy)
+        value_unit(0, 0, 0, scalar_copy)
+        value_unit(0, 1, 0, scalar_copy)
+        turned = turn_tokens(0, 3)
+        quantise_tokens(0, 2)
+        value_unit(0, 0, 1, scalar_copy)
+        value_unit(0, 1, 1, scalar_copy)
+        store(0, VALUE, 0, 0, TILES // 2)
+        sort_tokens(turned, 0, 3, 0, vector_copy)
+        sort_tokens(turned, 0, 3, 1, vector_copy)
+        turned = turn_weights(QUERY, 0)
+        sort_weights(turned, QUERY, 0, vector_copy)
+        quantise_tokens(0, 3)
+        quantise_weights(QUERY, 0, 2)
+        for c in range(2):
+            for h in (2, 3):
+                value_unit(0, h, c, scalar_copy)
+        store(0, VALUE, 2, 0, TILES // 2)
+        turned_query = turn_weights(QUERY, 2)
+
+        pairs = [(b, kind, h, c) for b in range(BATCH) for kind in (QUERY, KEY) for h in (0, 2) for c in range(CHUNKS)]
+        values = [(0, h + a, c) for h in (0, 2) for c in (2, 3) for a in (0, 1)]
+        values += [(1, h + a, c) for h in (0, 2) for c in range(CHUNKS) for a in (0, 1)]
+        rotary = project_rotary(*pairs[0])
+        for n, pair in enumerate(pairs):
+            b, kind, h, c = pair
+            next_rotary = project_rotary(*pairs[n + 1]) if n + 1 < len(pairs) else None
+            rotate(rotary, *pair)
+            plain_unit(*pair)
+            rotary = next_rotary
+            if b == 0 and n < HALVES and c % 2 == 1:
+                store(b, kind, h, c // 2 * TILES // 2, TILES // 2)
+            elif n >= HALVES and c == CHUNKS - 1:
+                store(b, kind, h, 0, TILES)
+            if n == 0:
+                sort_weights(turned_query, QUERY, 2, scalar_copy)
+            count = VALUES_BESIDE[n] if n < len(VALUES_BESIDE) else 1
+            for value in values[:count]:
+                value_unit(*value, scalar_copy)
+                vb, vh, vc = value
+                if vh % 2 == 1 and vc == CHUNKS - 1:
+                    if vb == 0:
+                        store(0, VALUE, vh - 1, TILES // 2, TILES // 2)
+                    elif vh > VH:
+                        store(1, VALUE, vh - 1, 0, TILES)
+                    else:
+                        store(1, VALUE, vh - 1, TILES // 2, TILES // 2)
+                if vb == 1 and vh % 2 == 1 and vc == 1 and vh <= VH:
+                    store(1, VALUE, vh - 1, 0, TILES // 2)
+            values = values[count:]
+            if n == 2:
+                quantise_weights(QUERY, 2, 2)
+            if n == 3:
+                turned_weights = [turn_weights(KEY, 0), turn_weights(KEY, 2)]
+            if n == 4:
+                sort_weights(turned_weights[0], KEY, 0, scalar_copy)
+                sort_weights(turned_weights[1], KEY, 2, scalar_copy)
+            if n == 5:
+                quantise_weights(KEY, 0, HEADS)
+            if n in (5, 7, 9, 11):
+                turned = turn_tokens(1, (n - 5) // 2)
+            if n in (6, 8, 10, 12):
+                sort_tokens(turned, 1, (n - 6) // 2, 0, scalar_copy)
+                sort_tokens(turned, 1, (n - 6) // 2, 1, scalar_copy)
+            if n in (7, 9, 11, 13):
+                quantise_tokens(1, (n - 7) // 2)

@@ -20,12 +20,14 @@ PAIRS = ROTARY // 2
 ROPE_BASE = 10000.0
 VALUES_BESIDE = [0, 2, 2, 1, 1, 1, 1, 0, 0, 0, 1, 1, 1, 1]
 HALVES=16
-VH=0
+VH=1
 OUTPUT_OF = {0: 0, 1: 2, 2: 1}
 QUERY, VALUE, KEY = 0, 1, 2
 TILES = SEQ // P
 CHUNK = 4
 CHUNKS = TILES // CHUNK
+BANK = 512
+WARM_UPS = 5
 ROUND_MAGIC = 12582912.0
 COARSE_STEP = 2.0**-15
 DECADE = PAIRS // 4
@@ -119,6 +121,12 @@ def tile_ttcodegenattention_pa_t_kernel(tc, hidden_states, w_qkv, out_0, out_1, 
         nc.gpsimd.iota(position_int[:], pattern=[[1, TILES]], base=0, channel_multiplier=TILES)
         identity = const.tile([P, P], F32)
         make_identity(nc, identity[:])
+
+        idle = const.tile([P, BANK], BF16)
+        nc.vector.memset(idle[:], 0.0)
+        unread = banks.tile([P, BANK], F32, name="bank")
+        for _ in range(WARM_UPS):
+            nc.tensor.matmul(out=unread[:], lhsT=idle[:, :P], rhs=idle[:], start=True, stop=True)
 
         warm = const.tile([P, 1], F32)
         nc.vector.memset(warm[:], 0.0)

@@ -79,8 +79,8 @@ def reduced_angles(nc, pool, position_int):
 
 def rotation_factors(nc, pool, turns):
     sign = pool.tile([P, 2], F32)
-    nc.gpsimd.memset(sign[:, 0:1], 1.0)
-    nc.gpsimd.memset(sign[:, 1:2], -1.0)
+    nc.gpsimd.memset(sign[:, 0:1], -1.0)
+    nc.gpsimd.memset(sign[:, 1:2], 1.0)
     factors = pool.tile([P, TILES, 2, ROTARY], F32)
     shape = [P, TILES, PAIRS, 2]
     sine = pool.tile([P, TILES, PAIRS], F32)
@@ -263,17 +263,25 @@ def tile_ttcodegenattention_pa_t_kernel(tc, hidden_states, w_qkv, out_0, out_1, 
         def rotate(rotary, b, kind, h, c):
             rows = slice(c * CHUNK, (c + 1) * CHUNK)
             products = products_pool.tile([P, CHUNK, 2, P], F32, name="products")
-            shape = [P, CHUNK, 2, 2, ROTARY]
-            nc.vector.tensor_tensor(
-                out=products[:].rearrange("p t k (h d) -> p t k h d", h=2),
-                in0=rotary[:].rearrange("p t (h d) -> p t h d", h=2).unsqueeze(2).to_broadcast(shape),
-                in1=factors[:, rows, :, :].unsqueeze(3).to_broadcast(shape),
-                op=ALU.mult,
-            )
+            by_head = rotary[:].rearrange("p t (h d) -> p t h d", h=2)
+            by_pair = rotary[:].rearrange("p t (h i e) -> p t h i e", h=2, e=2)
+            for k in range(2):
+                table = factors[:, rows, k, :].unsqueeze(2).to_broadcast([P, CHUNK, 2, ROTARY])
+                if k == 0:
+                    nc.vector.tensor_tensor(
+                        out=products[:, :, k, :].rearrange("p t (h d) -> p t h d", h=2), in0=by_head, in1=table, op=ALU.mult
+                    )
+                else:
+                    nc.vector.tensor_tensor(
+                        out=products[:, :, k, :].rearrange("p t (h i e) -> p t h i e", h=2, e=2),
+                        in0=by_pair[:, :, :, :, ::-1],
+                        in1=table.rearrange("p t h (i e) -> p t h i e", e=2),
+                        op=ALU.mult,
+                    )
             nc.gpsimd.tensor_tensor(
-                out=by_tile(b, kind, h, c)[:, :, :, :ROTARY].rearrange("p t h (i e) -> p t h i e", e=2),
-                in0=products[:, :, 0, :].rearrange("p t (h i e) -> p t h i e", h=2, e=2),
-                in1=products[:, :, 1, :].rearrange("p t (h i e) -> p t h i e", h=2, e=2)[:, :, :, :, ::-1],
+                out=by_tile(b, kind, h, c)[:, :, :, :ROTARY],
+                in0=products[:, :, 0, :].rearrange("p t (h d) -> p t h d", h=2),
+                in1=products[:, :, 1, :].rearrange("p t (h d) -> p t h d", h=2),
                 op=ALU.add,
             )
 

@@ -18,16 +18,11 @@ BATCH, SEQ, CHANNELS = 2, 2048, 512
 HEADS, HEAD_DIM, ROTARY = 4, 128, 64
 PAIRS = ROTARY // 2
 ROPE_BASE = 10000.0
-VALUES_BESIDE = [0, 2, 2, 1, 1, 1, 1, 0, 0, 0, 1, 1, 1, 1]
-HALVES=16
-VH=1
 OUTPUT_OF = {0: 0, 1: 2, 2: 1}
 QUERY, VALUE, KEY = 0, 1, 2
 TILES = SEQ // P
 CHUNK = 4
 CHUNKS = TILES // CHUNK
-BANK = 512
-WARM_UPS = 5
 ROUND_MAGIC = 12582912.0
 COARSE_STEP = 2.0**-15
 DECADE = PAIRS // 4
@@ -82,27 +77,30 @@ def rotation_factors(nc, pool, turns):
     nc.gpsimd.memset(sign[:, 0:1], -1.0)
     nc.gpsimd.memset(sign[:, 1:2], 1.0)
     factors = pool.tile([P, TILES, 2, ROTARY], F32)
-    shape = [P, TILES, PAIRS, 2]
     sine = pool.tile([P, TILES, PAIRS], F32)
     half_sine = pool.tile([P, TILES, PAIRS], F32)
     squared = pool.tile([P, TILES, PAIRS], F32)
     nc.scalar.activation(out=half_sine[:], in_=turns[:], func=ACT.Sin, scale=math.pi)
     nc.scalar.activation(out=sine[:], in_=turns[:], func=ACT.Sin, scale=2.0 * math.pi)
-    nc.gpsimd.tensor_tensor(out=squared[:], in0=half_sine[:], in1=half_sine[:], op=ALU.mult)
-    nc.gpsimd.tensor_scalar(
-        out=factors[:, :, 0, :].rearrange("p t (i e) -> p t i e", e=2),
-        in0=squared[:].unsqueeze(3).to_broadcast(shape),
-        scalar1=-2.0,
-        scalar2=1.0,
-        op0=ALU.mult,
-        op1=ALU.add,
-    )
-    nc.gpsimd.tensor_tensor(
-        out=factors[:, :, 1, :].rearrange("p t (i e) -> p t i e", e=2),
-        in0=sine[:].unsqueeze(3).to_broadcast(shape),
-        in1=sign[:].unsqueeze(1).unsqueeze(1).to_broadcast(shape),
-        op=ALU.mult,
-    )
+    for rows in (slice(0, TILES // 2), slice(TILES // 2, TILES)):
+        shape = [P, TILES // 2, PAIRS, 2]
+        nc.gpsimd.tensor_tensor(
+            out=squared[:, rows, :], in0=half_sine[:, rows, :], in1=half_sine[:, rows, :], op=ALU.mult
+        )
+        nc.gpsimd.tensor_scalar(
+            out=factors[:, rows, 0, :].rearrange("p t (i e) -> p t i e", e=2),
+            in0=squared[:, rows, :].unsqueeze(3).to_broadcast(shape),
+            scalar1=-2.0,
+            scalar2=1.0,
+            op0=ALU.mult,
+            op1=ALU.add,
+        )
+        nc.gpsimd.tensor_tensor(
+            out=factors[:, rows, 1, :].rearrange("p t (i e) -> p t i e", e=2),
+            in0=sine[:, rows, :].unsqueeze(3).to_broadcast(shape),
+            in1=sign[:].unsqueeze(1).unsqueeze(1).to_broadcast(shape),
+            op=ALU.mult,
+        )
     return factors
 
 
@@ -122,12 +120,6 @@ def tile_ttcodegenattention_pa_t_kernel(tc, hidden_states, w_qkv, out_0, out_1, 
         identity = const.tile([P, P], F32)
         make_identity(nc, identity[:])
 
-        idle = const.tile([P, BANK], BF16)
-        nc.vector.memset(idle[:], 0.0)
-        unread = banks.tile([P, BANK], F32, name="bank")
-        for _ in range(WARM_UPS):
-            nc.tensor.matmul(out=unread[:], lhsT=idle[:, :P], rhs=idle[:], start=True, stop=True)
-
         warm = const.tile([P, 1], F32)
         nc.vector.memset(warm[:], 0.0)
         nc.scalar.activation(out=warm[:], in_=warm[:], func=ACT.Sin)
@@ -146,12 +138,13 @@ def tile_ttcodegenattention_pa_t_kernel(tc, hidden_states, w_qkv, out_0, out_1, 
 
         load_tokens(0, 0, CHUNK)
         load_weights(VALUE)
-        for c in range(1, CHUNKS):
-            load_tokens(0, c * CHUNK, CHUNK)
+        load_tokens(0, CHUNK, CHUNK)
         load_weights(QUERY)
+        load_tokens(0, 2 * CHUNK, CHUNK)
+        load_tokens(0, 3 * CHUNK, CHUNK)
         load_weights(KEY)
-        for half in range(2):
-            load_tokens(1, half * TILES // 2, TILES // 2)
+        for first in (0, TILES // 2):
+            load_tokens(1, first, TILES // 2)
 
         turns = reduced_angles(nc, const, position_int)
 
@@ -293,6 +286,8 @@ def tile_ttcodegenattention_pa_t_kernel(tc, hidden_states, w_qkv, out_0, out_1, 
             )
 
         scalar_copy, vector_copy = copy_out
+        half = TILES // 2
+        pairs = [(b, kind, h, c) for b in range(BATCH) for kind in (QUERY, KEY) for h in (0, 2) for c in range(CHUNKS)]
 
         turned = turn_tokens(0, 0)
         sort_tokens(turned, 0, 0, 0, scalar_copy)
@@ -306,72 +301,70 @@ def tile_ttcodegenattention_pa_t_kernel(tc, hidden_states, w_qkv, out_0, out_1, 
         sort_tokens(turned, 0, 1, 0, scalar_copy)
         quantise_weights(VALUE, 0, HEADS)
         sort_tokens(turned, 0, 1, 1, vector_copy)
-        turned = turn_tokens(0, 2)
-        sort_tokens(turned, 0, 2, 0, scalar_copy)
+        turned_query = turn_weights(QUERY, 0)
+        sort_weights(turned_query, QUERY, 0, vector_copy)
         quantise_tokens(0, 1)
-        sort_tokens(turned, 0, 2, 1, vector_copy)
         value_unit(0, 0, 0, scalar_copy)
         value_unit(0, 1, 0, scalar_copy)
-        turned = turn_tokens(0, 3)
-        quantise_tokens(0, 2)
+        quantise_weights(QUERY, 0, 2)
+        turned = turn_tokens(0, 2)
+        rotaries = [project_rotary(*pair) for pair in pairs[:2]]
+        sort_tokens(turned, 0, 2, 0, scalar_copy)
+        sort_tokens(turned, 0, 2, 1, scalar_copy)
         value_unit(0, 0, 1, scalar_copy)
         value_unit(0, 1, 1, scalar_copy)
-        store(0, VALUE, 0, 0, TILES // 2)
+        store(0, VALUE, 0, 0, half)
+        turned = turn_tokens(0, 3)
+        for rotary, pair in zip(rotaries, pairs[:2]):
+            rotate(rotary, *pair)
+            plain_unit(*pair)
+        store(0, QUERY, 0, 0, half)
+        quantise_tokens(0, 2)
         sort_tokens(turned, 0, 3, 0, vector_copy)
         sort_tokens(turned, 0, 3, 1, vector_copy)
-        turned = turn_weights(QUERY, 0)
-        sort_weights(turned, QUERY, 0, vector_copy)
+        rotary = project_rotary(*pairs[2])
         quantise_tokens(0, 3)
-        quantise_weights(QUERY, 0, 2)
         for c in range(2):
             for h in (2, 3):
                 value_unit(0, h, c, scalar_copy)
-        store(0, VALUE, 2, 0, TILES // 2)
+        store(0, VALUE, 2, 0, half)
         turned_query = turn_weights(QUERY, 2)
 
-        pairs = [(b, kind, h, c) for b in range(BATCH) for kind in (QUERY, KEY) for h in (0, 2) for c in range(CHUNKS)]
         values = [(0, h + a, c) for h in (0, 2) for c in (2, 3) for a in (0, 1)]
         values += [(1, h + a, c) for h in (0, 2) for c in range(CHUNKS) for a in (0, 1)]
-        rotary = project_rotary(*pairs[0])
+        beside = [0,0,1,1,1,1,1,1,1,0,1,0,1,0,1,1]
         for n, pair in enumerate(pairs):
+            if n < 2:
+                continue
             b, kind, h, c = pair
-            next_rotary = project_rotary(*pairs[n + 1]) if n + 1 < len(pairs) else None
             rotate(rotary, *pair)
             plain_unit(*pair)
-            rotary = next_rotary
-            if b == 0 and n < HALVES and c % 2 == 1:
-                store(b, kind, h, c // 2 * TILES // 2, TILES // 2)
-            elif n >= HALVES and c == CHUNKS - 1:
+            if n == 2:
+                sort_weights(turned_query, QUERY, 2, vector_copy)
+                quantise_weights(QUERY, 2, 2)
+            rotary = project_rotary(*pairs[n + 1]) if n + 1 < len(pairs) else None
+            if n < 24 and c % 2 == 1:
+                store(b, kind, h, (c - 1) * CHUNK, half)
+            elif n >= 24 and c == CHUNKS - 1:
                 store(b, kind, h, 0, TILES)
-            if n == 0:
-                sort_weights(turned_query, QUERY, 2, scalar_copy)
-            count = VALUES_BESIDE[n] if n < len(VALUES_BESIDE) else 1
+            count = beside[n] if n < len(beside) else 1
             for value in values[:count]:
                 value_unit(*value, scalar_copy)
                 vb, vh, vc = value
-                if vh % 2 == 1 and vc == CHUNKS - 1:
-                    if vb == 0:
-                        store(0, VALUE, vh - 1, TILES // 2, TILES // 2)
-                    elif vh > VH:
-                        store(1, VALUE, vh - 1, 0, TILES)
-                    else:
-                        store(1, VALUE, vh - 1, TILES // 2, TILES // 2)
-                if vb == 1 and vh % 2 == 1 and vc == 1 and vh <= VH:
-                    store(1, VALUE, vh - 1, 0, TILES // 2)
+                if vh % 2 == 1 and vc % 2 == 1:
+                    store(vb, VALUE, vh - 1, (vc - 1) * CHUNK, half)
             values = values[count:]
-            if n == 2:
-                quantise_weights(QUERY, 2, 2)
             if n == 3:
                 turned_weights = [turn_weights(KEY, 0), turn_weights(KEY, 2)]
-            if n == 4:
+            if n == 3 + 1:
                 sort_weights(turned_weights[0], KEY, 0, scalar_copy)
                 sort_weights(turned_weights[1], KEY, 2, scalar_copy)
-            if n == 5:
+            if n == 3 + 2:
                 quantise_weights(KEY, 0, HEADS)
-            if n in (5, 7, 9, 11):
-                turned = turn_tokens(1, (n - 5) // 2)
-            if n in (6, 8, 10, 12):
-                sort_tokens(turned, 1, (n - 6) // 2, 0, scalar_copy)
-                sort_tokens(turned, 1, (n - 6) // 2, 1, scalar_copy)
-            if n in (7, 9, 11, 13):
-                quantise_tokens(1, (n - 7) // 2)
+            if n - 1 in (8, 10, 12, 13):
+                sort_tokens(turned, 1, (8, 10, 12, 13).index(n - 1), 0, scalar_copy)
+                sort_tokens(turned, 1, (8, 10, 12, 13).index(n - 1), 1, scalar_copy)
+            if n - 2 in (8, 10, 12, 13):
+                quantise_tokens(1, (8, 10, 12, 13).index(n - 2))
+            if n in (8, 10, 12, 13):
+                turned = turn_tokens(1, (8, 10, 12, 13).index(n))

@@ -74,8 +74,8 @@ def reduced_angles(nc, pool, position_int):
 
 def rotation_factors(nc, pool, turns):
     sign = pool.tile([P, 2], F32)
-    nc.gpsimd.memset(sign[:, 0:1], -1.0)
-    nc.gpsimd.memset(sign[:, 1:2], 1.0)
+    nc.gpsimd.memset(sign[:, 0:1], 1.0)
+    nc.gpsimd.memset(sign[:, 1:2], -1.0)
     factors = pool.tile([P, TILES, 2, ROTARY], F32)
     sine = pool.tile([P, TILES, PAIRS], F32)
     half_sine = pool.tile([P, TILES, PAIRS], F32)
@@ -237,7 +237,8 @@ def tile_ttcodegenattention_pa_t_kernel(tc, hidden_states, w_qkv, out_0, out_1, 
         def store(b, kind, h, first, count):
             rows = slice(first, first + count)
             view = out_views[OUTPUT_OF[kind]][b]
-            nc.sync.dma_start(out=view[:, h : h + 2, rows, :], in_=stage_of(b, kind, h)[:, :, rows, :])
+            for a in range(2):
+                nc.sync.dma_start(out=view[:, h + a, rows, :], in_=stage_of(b, kind, h)[:, a, rows, :])
 
         def value_unit(b, h, c, copy):
             pair, head = h // 2 * 2, h % 2
@@ -256,25 +257,17 @@ def tile_ttcodegenattention_pa_t_kernel(tc, hidden_states, w_qkv, out_0, out_1, 
         def rotate(rotary, b, kind, h, c):
             rows = slice(c * CHUNK, (c + 1) * CHUNK)
             products = products_pool.tile([P, CHUNK, 2, P], F32, name="products")
-            by_head = rotary[:].rearrange("p t (h d) -> p t h d", h=2)
-            by_pair = rotary[:].rearrange("p t (h i e) -> p t h i e", h=2, e=2)
-            for k in range(2):
-                table = factors[:, rows, k, :].unsqueeze(2).to_broadcast([P, CHUNK, 2, ROTARY])
-                if k == 0:
-                    nc.vector.tensor_tensor(
-                        out=products[:, :, k, :].rearrange("p t (h d) -> p t h d", h=2), in0=by_head, in1=table, op=ALU.mult
-                    )
-                else:
-                    nc.vector.tensor_tensor(
-                        out=products[:, :, k, :].rearrange("p t (h i e) -> p t h i e", h=2, e=2),
-                        in0=by_pair[:, :, :, :, ::-1],
-                        in1=table.rearrange("p t h (i e) -> p t h i e", e=2),
-                        op=ALU.mult,
-                    )
+            shape = [P, CHUNK, 2, 2, ROTARY]
+            nc.vector.tensor_tensor(
+                out=products[:].rearrange("p t k (h d) -> p t k h d", h=2),
+                in0=rotary[:].rearrange("p t (h d) -> p t h d", h=2).unsqueeze(2).to_broadcast(shape),
+                in1=factors[:, rows, :, :].unsqueeze(3).to_broadcast(shape),
+                op=ALU.mult,
+            )
             nc.gpsimd.tensor_tensor(
-                out=by_tile(b, kind, h, c)[:, :, :, :ROTARY],
-                in0=products[:, :, 0, :].rearrange("p t (h d) -> p t h d", h=2),
-                in1=products[:, :, 1, :].rearrange("p t (h d) -> p t h d", h=2),
+                out=by_tile(b, kind, h, c)[:, :, :, :ROTARY].rearrange("p t h (i e) -> p t h i e", e=2),
+                in0=products[:, :, 0, :].rearrange("p t (h i e) -> p t h i e", h=2, e=2),
+                in1=products[:, :, 1, :].rearrange("p t (h i e) -> p t h i e", h=2, e=2)[:, :, :, :, ::-1],
                 op=ALU.add,
             )
 
@@ -343,16 +336,19 @@ def tile_ttcodegenattention_pa_t_kernel(tc, hidden_states, w_qkv, out_0, out_1, 
                 sort_weights(turned_query, QUERY, 2, vector_copy)
                 quantise_weights(QUERY, 2, 2)
             rotary = project_rotary(*pairs[n + 1]) if n + 1 < len(pairs) else None
-            if n < 24 and c % 2 == 1:
+            if n < 20 and c % 2 == 1:
                 store(b, kind, h, (c - 1) * CHUNK, half)
-            elif n >= 24 and c == CHUNKS - 1:
+            elif n >= 20 and c == CHUNKS - 1:
                 store(b, kind, h, 0, TILES)
             count = beside[n] if n < len(beside) else 1
             for value in values[:count]:
                 value_unit(*value, scalar_copy)
                 vb, vh, vc = value
-                if vh % 2 == 1 and vc % 2 == 1:
-                    store(vb, VALUE, vh - 1, (vc - 1) * CHUNK, half)
+                if vh % 2 == 1:
+                    if vb == 0 and vc % 2 == 1:
+                        store(vb, VALUE, vh - 1, (vc - 1) * CHUNK, half)
+                    elif vb == 1 and vc == CHUNKS - 1:
+                        store(vb, VALUE, vh - 1, 0, TILES)
             values = values[count:]
             if n == 3:
                 turned_weights = [turn_weights(KEY, 0), turn_weights(KEY, 2)]

@@ -22,7 +22,10 @@ OUTPUT_OF = {0: 0, 1: 2, 2: 1}
 QUERY, VALUE, KEY = 0, 1, 2
 TILES = SEQ // P
 CHUNK = 4
+UNIT = 2
+UNITS = TILES // UNIT
 CHUNKS = TILES // CHUNK
+HALF = TILES // 2
 ROUND_MAGIC = 12582912.0
 COARSE_STEP = 2.0**-15
 DECADE = PAIRS // 4
@@ -173,18 +176,15 @@ def tile_ttcodegenattention_pa_t_kernel(tc, hidden_states, w_qkv, out_0, out_1, 
                     in_=turned[:].rearrange("p a u d -> p a d u"),
                 )
             else:
+                by_half = weights_grouped[:, kind, :, :].bitcast(F32).rearrange("p (r a d) u -> p r a d u", r=2, a=HEADS)
                 for a in range(2):
-                    copy(
-                        out=columns.rearrange("p (r a d) u -> p r a d u", r=2, a=2)[:, :, a, :, :],
-                        in_=turned[:, a, :, :].rearrange("p u (r d) -> p r d u", r=2),
-                    )
+                    copy(out=by_half[:, :, h + a, :, :], in_=turned[:, a, :, :].rearrange("p u (r d) -> p r d u", r=2))
 
-        def quantise_weights(kind, first, heads):
-            columns = slice(first * HEAD_DIM, (first + heads) * HEAD_DIM)
+        def quantise_weights(kind):
             nc.vector.quantize_mx(
-                out=weights_codes[:, kind, columns].bitcast(FP8X4),
-                scales=weights_scales[:, kind, columns],
-                in_=weights_grouped[:, kind, columns, :].rearrange("p n v -> p (n v)"),
+                out=weights_codes[:, kind, :].bitcast(FP8X4),
+                scales=weights_scales[:, kind, :],
+                in_=weights_grouped[:, kind, :, :].rearrange("p n v -> p (n v)"),
             )
 
         token_codes = [const.tile([P, TILES, P], U32, align_bytes=64, name="codes%d" % b) for b in range(BATCH)]
@@ -212,75 +212,78 @@ def tile_ttcodegenattention_pa_t_kernel(tc, hidden_states, w_qkv, out_0, out_1, 
                 in_=grouped_tokens[(b, c)][:].rearrange("p a r v -> p (a r v)"),
             )
 
-        def project(result, b, c, kind, group):
-            columns = slice(group * P, (group + 1) * P)
-            for a in range(CHUNK):
-                t = c * CHUNK + a
-                nc.tensor.matmul_mx(
-                    out=result[:, a, :],
-                    lhsT=token_codes[b][:, t, :].bitcast(FP8X4),
-                    lhsT_scale=token_scales[b][:, t, :],
-                    rhs=weights_codes[:, kind, columns].bitcast(FP8X4),
-                    rhs_scale=weights_scales[:, kind, columns],
-                    start=True,
-                    stop=True,
-                )
+        def project(out, b, t, kind, first, count):
+            columns = slice(first, first + count)
+            nc.tensor.matmul_mx(
+                out=out,
+                lhsT=token_codes[b][:, t, :].bitcast(FP8X4),
+                lhsT_scale=token_scales[b][:, t, :],
+                rhs=weights_codes[:, kind, columns].bitcast(FP8X4),
+                rhs_scale=weights_scales[:, kind, columns],
+                start=True,
+                stop=True,
+            )
 
         out_views = [o.rearrange("b h (p t) d -> b p h t d", t=TILES) for o in (out_0, out_1, out_2)]
         staged = {}
 
-        def stage_of(b, kind, h):
-            if (b, kind, h) not in staged:
-                staged[(b, kind, h)] = stages.tile([P, 2, TILES, HEAD_DIM], F32, name="stage")
-            return staged[(b, kind, h)]
+        def stage_of(b, kind, t):
+            key = (b, kind, t // HALF)
+            if key not in staged:
+                staged[key] = stages.tile([P, HEADS, HALF, HEAD_DIM], F32, name="stage")
+            return staged[key]
 
-        def store(b, kind, h, first, count):
-            rows = slice(first, first + count)
-            view = out_views[OUTPUT_OF[kind]][b]
-            for a in range(2):
-                nc.sync.dma_start(out=view[:, h + a, rows, :], in_=stage_of(b, kind, h)[:, a, rows, :])
+        def store(b, kind, first, count):
+            nc.sync.dma_start(
+                out=out_views[OUTPUT_OF[kind]][b][:, :, first : first + count, :],
+                in_=stage_of(b, kind, first)[:, :, first % HALF : first % HALF + count, :],
+            )
 
-        def value_unit(b, h, c, copy):
-            pair, head = h // 2 * 2, h % 2
-            value = banks.tile([P, CHUNK, P], F32, name="bank")
-            project(value, b, c, VALUE, h)
-            copy(out=stage_of(b, VALUE, pair)[:, head, c * CHUNK : (c + 1) * CHUNK, :], in_=value[:])
+        def value_unit(b, t):
+            value = banks.tile([P, HEADS * HEAD_DIM], F32, name="bank")
+            project(value[:], b, t, VALUE, 0, HEADS * HEAD_DIM)
+            nc.scalar.copy(
+                out=stage_of(b, VALUE, t)[:, :, t % HALF, :], in_=value[:].rearrange("p (h d) -> p h d", h=HEADS)
+            )
 
-        def project_rotary(b, kind, h, c):
-            rotary = banks.tile([P, CHUNK, P], F32, name="bank")
-            project(rotary, b, c, kind, h)
-            return rotary
+        def project_half(b, kind, u, first):
+            bank = banks.tile([P, UNIT, HEADS * ROTARY], F32, name="bank")
+            for a in range(UNIT):
+                project(bank[:, a, :], b, u * UNIT + a, kind, first, HEADS * ROTARY)
+            return bank
 
-        def by_tile(b, kind, h, c):
-            return stage_of(b, kind, h)[:, :, c * CHUNK : (c + 1) * CHUNK, :].rearrange("p h t d -> p t h d")
+        def project_rotary(b, kind, u):
+            return project_half(b, kind, u, 0)
 
-        def rotate(rotary, b, kind, h, c):
-            rows = slice(c * CHUNK, (c + 1) * CHUNK)
-            products = products_pool.tile([P, CHUNK, 2, P], F32, name="products")
-            shape = [P, CHUNK, 2, 2, ROTARY]
+        def by_tile(b, kind, u):
+            first = u * UNIT % HALF
+            return stage_of(b, kind, u * UNIT)[:, :, first : first + UNIT, :].rearrange("p h t d -> p t h d")
+
+        def rotate(rotary, b, kind, u):
+            rows = slice(u * UNIT, (u + 1) * UNIT)
+            products = products_pool.tile([P, UNIT, 2, HEADS * ROTARY], F32, name="products")
+            shape = [P, UNIT, 2, HEADS, ROTARY]
             nc.vector.tensor_tensor(
-                out=products[:].rearrange("p t k (h d) -> p t k h d", h=2),
-                in0=rotary[:].rearrange("p t (h d) -> p t h d", h=2).unsqueeze(2).to_broadcast(shape),
+                out=products[:].rearrange("p t k (h d) -> p t k h d", h=HEADS),
+                in0=rotary[:].rearrange("p t (h d) -> p t h d", h=HEADS).unsqueeze(2).to_broadcast(shape),
                 in1=factors[:, rows, :, :].unsqueeze(3).to_broadcast(shape),
                 op=ALU.mult,
             )
             nc.gpsimd.tensor_tensor(
-                out=by_tile(b, kind, h, c)[:, :, :, :ROTARY].rearrange("p t h (i e) -> p t h i e", e=2),
-                in0=products[:, :, 0, :].rearrange("p t (h i e) -> p t h i e", h=2, e=2),
-                in1=products[:, :, 1, :].rearrange("p t (h i e) -> p t h i e", h=2, e=2)[:, :, :, :, ::-1],
+                out=by_tile(b, kind, u)[:, :, :, :ROTARY].rearrange("p t h (i e) -> p t h i e", e=2),
+                in0=products[:, :, 0, :].rearrange("p t (h i e) -> p t h i e", h=HEADS, e=2),
+                in1=products[:, :, 1, :].rearrange("p t (h i e) -> p t h i e", h=HEADS, e=2)[:, :, :, :, ::-1],
                 op=ALU.add,
             )
 
-        def plain_unit(b, kind, h, c):
-            plain = banks.tile([P, CHUNK, P], F32, name="bank")
-            project(plain, b, c, kind, h + 1)
+        def plain_unit(b, kind, u):
+            plain = project_half(b, kind, u, HEADS * ROTARY)
             nc.scalar.copy(
-                out=by_tile(b, kind, h, c)[:, :, :, ROTARY:], in_=plain[:].rearrange("p t (h d) -> p t h d", h=2)
+                out=by_tile(b, kind, u)[:, :, :, ROTARY:], in_=plain[:].rearrange("p t (h d) -> p t h d", h=HEADS)
             )
 
         scalar_copy, vector_copy = copy_out
-        half = TILES // 2
-        pairs = [(b, kind, h, c) for b in range(BATCH) for kind in (QUERY, KEY) for h in (0, 2) for c in range(CHUNKS)]
+        units = [(b, kind, u) for b in range(BATCH) for kind in (QUERY, KEY) for u in range(UNITS)]
 
         turned = turn_tokens(0, 0)
         sort_tokens(turned, 0, 0, 0, scalar_copy)
@@ -292,75 +295,65 @@ def tile_ttcodegenattention_pa_t_kernel(tc, hidden_states, w_qkv, out_0, out_1, 
         sort_weights(turned_weights[1], VALUE, 2, vector_copy)
         turned = turn_tokens(0, 1)
         sort_tokens(turned, 0, 1, 0, scalar_copy)
-        quantise_weights(VALUE, 0, HEADS)
+        quantise_weights(VALUE)
         sort_tokens(turned, 0, 1, 1, vector_copy)
-        turned_query = turn_weights(QUERY, 0)
-        sort_weights(turned_query, QUERY, 0, vector_copy)
+        turned_query = [turn_weights(QUERY, 0), turn_weights(QUERY, 2)]
+        sort_weights(turned_query[0], QUERY, 0, vector_copy)
         quantise_tokens(0, 1)
-        value_unit(0, 0, 0, scalar_copy)
-        value_unit(0, 1, 0, scalar_copy)
-        quantise_weights(QUERY, 0, 2)
+        value_unit(0, 0)
+        sort_weights(turned_query[1], QUERY, 2, vector_copy)
+        value_unit(0, 1)
+        value_unit(0, 2)
+        value_unit(0, 3)
+        store(0, VALUE, 0, CHUNK)
+        quantise_weights(QUERY)
+        rotaries = [project_rotary(*unit) for unit in units[:2]]
         turned = turn_tokens(0, 2)
-        rotaries = [project_rotary(*pair) for pair in pairs[:2]]
-        sort_tokens(turned, 0, 2, 0, scalar_copy)
+        for rotary, unit in zip(rotaries, units[:2]):
+            rotate(rotary, *unit)
+            plain_unit(*unit)
+        store(0, QUERY, 0, CHUNK)
+        sort_tokens(turned, 0, 2, 0, vector_copy)
         sort_tokens(turned, 0, 2, 1, scalar_copy)
-        value_unit(0, 0, 1, scalar_copy)
-        value_unit(0, 1, 1, scalar_copy)
-        store(0, VALUE, 0, 0, half)
-        turned = turn_tokens(0, 3)
-        for rotary, pair in zip(rotaries, pairs[:2]):
-            rotate(rotary, *pair)
-            plain_unit(*pair)
-        store(0, QUERY, 0, 0, half)
+        rotary = project_rotary(*units[2])
+        for t in range(CHUNK, 2 * CHUNK):
+            value_unit(0, t)
+        store(0, VALUE, CHUNK, CHUNK)
         quantise_tokens(0, 2)
-        sort_tokens(turned, 0, 3, 0, vector_copy)
-        sort_tokens(turned, 0, 3, 1, vector_copy)
-        rotary = project_rotary(*pairs[2])
-        quantise_tokens(0, 3)
-        for c in range(2):
-            for h in (2, 3):
-                value_unit(0, h, c, scalar_copy)
-        store(0, VALUE, 2, 0, half)
-        turned_query = turn_weights(QUERY, 2)
 
-        values = [(0, h + a, c) for h in (0, 2) for c in (2, 3) for a in (0, 1)]
-        values += [(1, h + a, c) for h in (0, 2) for c in range(CHUNKS) for a in (0, 1)]
-        beside = [0,0,1,1,1,1,1,1,1,0,1,0,1,0,1,1]
-        for n, pair in enumerate(pairs):
+        values = [(0, t) for t in range(2 * CHUNK, TILES)] + [(1, t) for t in range(TILES)]
+        beside = [0,0,0,0,1,1,1,1,1,1,1,1,1,0,1,0]
+        chunks = {2: (0, 3), 9: (1, 0), 12: (1, 1), 15: (1, 2), 18: (1, 3)}
+        for n, unit in enumerate(units):
             if n < 2:
                 continue
-            b, kind, h, c = pair
-            rotate(rotary, *pair)
-            plain_unit(*pair)
-            if n == 2:
-                sort_weights(turned_query, QUERY, 2, vector_copy)
-                quantise_weights(QUERY, 2, 2)
-            rotary = project_rotary(*pairs[n + 1]) if n + 1 < len(pairs) else None
-            if n < 20 and c % 2 == 1:
-                store(b, kind, h, (c - 1) * CHUNK, half)
-            elif n >= 20 and c == CHUNKS - 1:
-                store(b, kind, h, 0, TILES)
+            b, kind, u = unit
+            rotate(rotary, *unit)
+            plain_unit(*unit)
+            rotary = project_rotary(*units[n + 1]) if n + 1 < len(units) else None
+            if n < 16 and u % 2 == 1:
+                store(b, kind, (u - 1) * UNIT, CHUNK)
+            elif n >= 16 and u % 4 == 3:
+                store(b, kind, (u - 3) * UNIT, HALF)
             count = beside[n] if n < len(beside) else 1
-            for value in values[:count]:
-                value_unit(*value, scalar_copy)
-                vb, vh, vc = value
-                if vh % 2 == 1:
-                    if vb == 0 and vc % 2 == 1:
-                        store(vb, VALUE, vh - 1, (vc - 1) * CHUNK, half)
-                    elif vb == 1 and vc == CHUNKS - 1:
-                        store(vb, VALUE, vh - 1, 0, TILES)
+            for vb, t in values[:count]:
+                value_unit(vb, t)
+                if vb == 0 and t % CHUNK == CHUNK - 1:
+                    store(vb, VALUE, t - CHUNK + 1, CHUNK)
+                elif vb == 1 and t % HALF == HALF - 1:
+                    store(vb, VALUE, t - HALF + 1, HALF)
             values = values[count:]
-            if n == 3:
+            if n == 4:
                 turned_weights = [turn_weights(KEY, 0), turn_weights(KEY, 2)]
-            if n == 3 + 1:
+            if n == 5:
                 sort_weights(turned_weights[0], KEY, 0, scalar_copy)
-                sort_weights(turned_weights[1], KEY, 2, scalar_copy)
-            if n == 3 + 2:
-                quantise_weights(KEY, 0, HEADS)
-            if n - 1 in (8, 10, 12, 13):
-                sort_tokens(turned, 1, (8, 10, 12, 13).index(n - 1), 0, scalar_copy)
-                sort_tokens(turned, 1, (8, 10, 12, 13).index(n - 1), 1, scalar_copy)
-            if n - 2 in (8, 10, 12, 13):
-                quantise_tokens(1, (8, 10, 12, 13).index(n - 2))
-            if n in (8, 10, 12, 13):
-                turned = turn_tokens(1, (8, 10, 12, 13).index(n))
+                sort_weights(turned_weights[1], KEY, 2, vector_copy)
+            if n == 6:
+                quantise_weights(KEY)
+            if n - 1 in chunks:
+                for half in range(2):
+                    sort_tokens(turned, *chunks[n - 1], half, (scalar_copy if half else vector_copy))
+            if n - 2 in chunks:
+                quantise_tokens(*chunks[n - 2])
+            if n in chunks:
+                turned = turn_tokens(*chunks[n])

import math
from contextlib import ExitStack

import concourse.mybir as mybir
from concourse.masks import make_identity

F32 = mybir.dt.float32
BF16 = mybir.dt.bfloat16
I32 = mybir.dt.int32
U32 = mybir.dt.uint32
U8 = mybir.dt.uint8
FP8X4 = mybir.dt.float8_e4m3fn_x4
ALU = mybir.AluOpType
ACT = mybir.ActivationFunctionType

P = 128
BATCH, SEQ, CHANNELS = 2, 2048, 512
HEADS, HEAD_DIM, ROTARY = 4, 128, 64
PAIRS = ROTARY // 2
ROPE_BASE = 10000.0
OUTPUT_OF = {0: 0, 1: 2, 2: 1}
QUERY, VALUE, KEY = 0, 1, 2
TILES = SEQ // P
CHUNK = 4
UNIT = 2
UNITS = TILES // UNIT
CHUNKS = TILES // CHUNK
HALF = TILES // 2
ROUND_MAGIC = 12582912.0
COARSE_STEP = 2.0**-15
DECADE = PAIRS // 4
WHOLE_PAIRS = 23
SPLIT_PAIRS = 12

FLOPS = 2 * BATCH * SEQ * CHANNELS * 3 * CHANNELS


def reduced_angles(nc, pool, position_int):
    position = pool.tile([P, TILES], F32)
    nc.vector.tensor_copy(out=position[:], in_=position_int[:])

    turns = pool.tile([P, TILES, PAIRS], F32)
    rest = pool.tile([P, TILES, SPLIT_PAIRS], F32)
    for i in range(PAIRS):
        frequency = ROPE_BASE ** (-i / PAIRS) / (2.0 * math.pi)
        if i < SPLIT_PAIRS:
            coarse = round(frequency / COARSE_STEP) * COARSE_STEP
            nc.vector.tensor_scalar_mul(out=turns[:, :, i], in0=position[:], scalar1=coarse)
            nc.scalar.mul(out=rest[:, :, i], in_=position[:], mul=frequency - coarse)
        elif i < SPLIT_PAIRS + DECADE:
            nc.vector.tensor_scalar_mul(out=turns[:, :, i], in0=position[:], scalar1=frequency)
    for i in range(SPLIT_PAIRS + DECADE, PAIRS, DECADE):
        count = min(DECADE, PAIRS - i)
        nc.vector.tensor_scalar_mul(
            out=turns[:, :, i : i + count], in0=turns[:, :, i - DECADE : i - DECADE + count], scalar1=0.1
        )

    whole = pool.tile([P, TILES, PAIRS], F32)

    def drop_whole_turns(count):
        nc.vector.tensor_scalar(
            out=whole[:, :, :count],
            in0=turns[:, :, :count],
            scalar1=ROUND_MAGIC,
            scalar2=ROUND_MAGIC,
            op0=ALU.add,
            op1=ALU.subtract,
        )
        nc.vector.tensor_sub(out=turns[:, :, :count], in0=turns[:, :, :count], in1=whole[:, :, :count])

    drop_whole_turns(WHOLE_PAIRS)
    nc.vector.tensor_add(out=turns[:, :, :SPLIT_PAIRS], in0=turns[:, :, :SPLIT_PAIRS], in1=rest[:])
    drop_whole_turns(SPLIT_PAIRS)

    return turns


def rotation_factors(nc, pool, turns):
    sign = pool.tile([P, 2], F32)
    nc.gpsimd.memset(sign[:, 0:1], 1.0)
    nc.gpsimd.memset(sign[:, 1:2], -1.0)
    factors = pool.tile([P, TILES, 2, ROTARY], F32)
    sine = pool.tile([P, TILES, PAIRS], F32)
    half_sine = pool.tile([P, TILES, PAIRS], F32)
    squared = pool.tile([P, TILES, PAIRS], F32)
    nc.scalar.activation(out=half_sine[:], in_=turns[:], func=ACT.Sin, scale=math.pi)
    nc.scalar.activation(out=sine[:], in_=turns[:], func=ACT.Sin, scale=2.0 * math.pi)
    for rows in (slice(0, TILES // 2), slice(TILES // 2, TILES)):
        shape = [P, TILES // 2, PAIRS, 2]
        nc.gpsimd.tensor_tensor(
            out=squared[:, rows, :], in0=half_sine[:, rows, :], in1=half_sine[:, rows, :], op=ALU.mult
        )
        nc.gpsimd.tensor_scalar(
            out=factors[:, rows, 0, :].rearrange("p t (i e) -> p t i e", e=2),
            in0=squared[:, rows, :].unsqueeze(3).to_broadcast(shape),
            scalar1=-2.0,
            scalar2=1.0,
            op0=ALU.mult,
            op1=ALU.add,
        )
        nc.gpsimd.tensor_tensor(
            out=factors[:, rows, 1, :].rearrange("p t (i e) -> p t i e", e=2),
            in0=sine[:, rows, :].unsqueeze(3).to_broadcast(shape),
            in1=sign[:].unsqueeze(1).unsqueeze(1).to_broadcast(shape),
            op=ALU.mult,
        )
    return factors


def tile_ttcodegenattention_pa_t_kernel(tc, hidden_states, w_qkv, out_0, out_1, out_2):
    nc = tc.nc

    with ExitStack() as ctx:
        const = ctx.enter_context(tc.tile_pool(name="const", bufs=1))
        tokens_grouped = ctx.enter_context(tc.tile_pool(name="tokens_grouped", bufs=3))
        products_pool = ctx.enter_context(tc.tile_pool(name="products_pool", bufs=3))
        stages = ctx.enter_context(tc.tile_pool(name="stages", bufs=6))
        banks = ctx.enter_context(tc.psum_pool(name="banks_psum", bufs=8))
        ctx.enter_context(tc.manual_schedule())

        position_int = const.tile([P, TILES], I32)
        nc.gpsimd.iota(position_int[:], pattern=[[1, TILES]], base=0, channel_multiplier=TILES)
        identity = const.tile([P, P], F32)
        make_identity(nc, identity[:])

        warm = const.tile([P, 1], F32)
        nc.vector.memset(warm[:], 0.0)
        nc.scalar.activation(out=warm[:], in_=warm[:], func=ACT.Sin)

        weights_in = const.tile([P, 3, HEADS, CHANNELS], BF16)
        weights_by_kind = w_qkv.rearrange("(s c p) k -> c p s k", c=3, p=P)
        tokens_by_partition = hidden_states.rearrange("b (p t) k -> b p t k", t=TILES)
        raw_tokens = [const.tile([P, TILES, CHANNELS], BF16, name="raw%d" % b) for b in range(BATCH)]

        def load_weights(kind):
            nc.sync.dma_start(out=weights_in[:, kind, :, :], in_=weights_by_kind[kind])

        def load_tokens(b, first, count):
            rows = slice(first, first + count)
            nc.sync.dma_start(out=raw_tokens[b][:, rows, :], in_=tokens_by_partition[b][:, rows, :])

        load_tokens(0, 0, CHUNK)
        load_weights(VALUE)
        load_tokens(0, CHUNK, CHUNK)
        load_weights(QUERY)
        load_tokens(0, 2 * CHUNK, CHUNK)
        load_tokens(0, 3 * CHUNK, CHUNK)
        load_weights(KEY)
        for first in (0, TILES // 2):
            load_tokens(1, first, TILES // 2)

        turns = reduced_angles(nc, const, position_int)

        def turn_two_row_blocks(first, second):
            turned = banks.tile([P, 2, 2, P], F32, name="bank")
            for a, block in enumerate((first, second)):
                words = block.bitcast(F32)
                for u in range(2):
                    nc.tensor.transpose(out=turned[:, a, u, :], in_=words[:, u::2], identity=identity[:])
            return turned

        copy_out = (nc.scalar.copy, nc.vector.tensor_copy)

        weights_grouped = const.tile([P, 3, HEADS * HEAD_DIM, 4], BF16, align_bytes=64)
        weights_codes = const.tile([P, 3, HEADS * HEAD_DIM], U32, align_bytes=64)
        weights_scales = const.tile([P, 3, HEADS * HEAD_DIM], U8, align_bytes=64)

        def turn_weights(kind, h):
            return turn_two_row_blocks(weights_in[:, kind, h, :], weights_in[:, kind, h + 1, :])

        def sort_weights(turned, kind, h, copy):
            columns = weights_grouped[:, kind, h * HEAD_DIM : (h + 2) * HEAD_DIM, :].bitcast(F32)
            if kind == VALUE:
                copy(
                    out=columns.rearrange("p (a d) u -> p a d u", a=2),
                    in_=turned[:].rearrange("p a u d -> p a d u"),
                )
            else:
                by_half = weights_grouped[:, kind, :, :].bitcast(F32).rearrange("p (r a d) u -> p r a d u", r=2, a=HEADS)
                for a in range(2):
                    copy(out=by_half[:, :, h + a, :, :], in_=turned[:, a, :, :].rearrange("p u (r d) -> p r d u", r=2))

        def quantise_weights(kind):
            nc.vector.quantize_mx(
                out=weights_codes[:, kind, :].bitcast(FP8X4),
                scales=weights_scales[:, kind, :],
                in_=weights_grouped[:, kind, :, :].rearrange("p n v -> p (n v)"),
            )

        token_codes = [const.tile([P, TILES, P], U32, align_bytes=64, name="codes%d" % b) for b in range(BATCH)]
        token_scales = [const.tile([P, TILES, P], U8, align_bytes=64, name="scales%d" % b) for b in range(BATCH)]

        grouped_tokens = {}

        def turn_tokens(b, c):
            tiles = range(c * CHUNK, (c + 1) * CHUNK, 2)
            return [turn_two_row_blocks(raw_tokens[b][:, t, :], raw_tokens[b][:, t + 1, :]) for t in tiles]

        def sort_tokens(turned, b, c, half, copy):
            if half == 0:
                grouped_tokens[(b, c)] = tokens_grouped.tile([P, CHUNK, P, 4], BF16, align_bytes=64, name="grouped")
            copy(
                out=grouped_tokens[(b, c)][:, 2 * half : 2 * half + 2, :, :].bitcast(F32),
                in_=turned[half][:].rearrange("p a u r -> p a r u"),
            )

        def quantise_tokens(b, c):
            rows = slice(c * CHUNK, (c + 1) * CHUNK)
            nc.vector.quantize_mx(
                out=token_codes[b][:, rows, :].rearrange("p a r -> p (a r)").bitcast(FP8X4),
                scales=token_scales[b][:, rows, :].rearrange("p a r -> p (a r)"),
                in_=grouped_tokens[(b, c)][:].rearrange("p a r v -> p (a r v)"),
            )

        def project(out, b, t, kind, first, count):
            columns = slice(first, first + count)
            nc.tensor.matmul_mx(
                out=out,
                lhsT=token_codes[b][:, t, :].bitcast(FP8X4),
                lhsT_scale=token_scales[b][:, t, :],
                rhs=weights_codes[:, kind, columns].bitcast(FP8X4),
                rhs_scale=weights_scales[:, kind, columns],
                start=True,
                stop=True,
            )

        out_views = [o.rearrange("b h (p t) d -> b p h t d", t=TILES) for o in (out_0, out_1, out_2)]
        staged = {}

        def stage_of(b, kind, t):
            key = (b, kind, t // HALF)
            if key not in staged:
                staged[key] = stages.tile([P, HEADS, HALF, HEAD_DIM], F32, name="stage")
            return staged[key]

        def store(b, kind, first, count):
            nc.sync.dma_start(
                out=out_views[OUTPUT_OF[kind]][b][:, :, first : first + count, :],
                in_=stage_of(b, kind, first)[:, :, first % HALF : first % HALF + count, :],
            )

        def value_unit(b, t):
            value = banks.tile([P, HEADS * HEAD_DIM], F32, name="bank")
            project(value[:], b, t, VALUE, 0, HEADS * HEAD_DIM)
            nc.scalar.copy(
                out=stage_of(b, VALUE, t)[:, :, t % HALF, :], in_=value[:].rearrange("p (h d) -> p h d", h=HEADS)
            )

        def project_half(b, kind, u, first):
            bank = banks.tile([P, UNIT, HEADS * ROTARY], F32, name="bank")
            for a in range(UNIT):
                project(bank[:, a, :], b, u * UNIT + a, kind, first, HEADS * ROTARY)
            return bank

        def project_rotary(b, kind, u):
            return project_half(b, kind, u, 0)

        def by_tile(b, kind, u):
            first = u * UNIT % HALF
            return stage_of(b, kind, u * UNIT)[:, :, first : first + UNIT, :].rearrange("p h t d -> p t h d")

        def rotate(rotary, b, kind, u):
            rows = slice(u * UNIT, (u + 1) * UNIT)
            products = products_pool.tile([P, UNIT, 2, HEADS * ROTARY], F32, name="products")
            shape = [P, UNIT, 2, HEADS, ROTARY]
            nc.vector.tensor_tensor(
                out=products[:].rearrange("p t k (h d) -> p t k h d", h=HEADS),
                in0=rotary[:].rearrange("p t (h d) -> p t h d", h=HEADS).unsqueeze(2).to_broadcast(shape),
                in1=factors[:, rows, :, :].unsqueeze(3).to_broadcast(shape),
                op=ALU.mult,
            )
            nc.gpsimd.tensor_tensor(
                out=by_tile(b, kind, u)[:, :, :, :ROTARY].rearrange("p t h (i e) -> p t h i e", e=2),
                in0=products[:, :, 0, :].rearrange("p t (h i e) -> p t h i e", h=HEADS, e=2),
                in1=products[:, :, 1, :].rearrange("p t (h i e) -> p t h i e", h=HEADS, e=2)[:, :, :, :, ::-1],
                op=ALU.add,
            )

        def plain_unit(b, kind, u):
            plain = project_half(b, kind, u, HEADS * ROTARY)
            nc.scalar.copy(
                out=by_tile(b, kind, u)[:, :, :, ROTARY:], in_=plain[:].rearrange("p t (h d) -> p t h d", h=HEADS)
            )

        scalar_copy, vector_copy = copy_out
        units = [(b, kind, u) for b in range(BATCH) for kind in (QUERY, KEY) for u in range(UNITS)]

        turned = turn_tokens(0, 0)
        sort_tokens(turned, 0, 0, 0, scalar_copy)
        factors = rotation_factors(nc, const, turns)
        sort_tokens(turned, 0, 0, 1, vector_copy)
        turned_weights = [turn_weights(VALUE, 0), turn_weights(VALUE, 2)]
        sort_weights(turned_weights[0], VALUE, 0, scalar_copy)
        quantise_tokens(0, 0)
        sort_weights(turned_weights[1], VALUE, 2, vector_copy)
        turned = turn_tokens(0, 1)
        sort_tokens(turned, 0, 1, 0, scalar_copy)
        quantise_weights(VALUE)
        sort_tokens(turned, 0, 1, 1, vector_copy)
        turned_query = [turn_weights(QUERY, 0), turn_weights(QUERY, 2)]
        sort_weights(turned_query[0], QUERY, 0, vector_copy)
        quantise_tokens(0, 1)
        value_unit(0, 0)
        sort_weights(turned_query[1], QUERY, 2, vector_copy)
        value_unit(0, 1)
        value_unit(0, 2)
        value_unit(0, 3)
        store(0, VALUE, 0, CHUNK)
        quantise_weights(QUERY)
        rotaries = [project_rotary(*unit) for unit in units[:2]]
        turned = turn_tokens(0, 2)
        for rotary, unit in zip(rotaries, units[:2]):
            rotate(rotary, *unit)
            plain_unit(*unit)
        store(0, QUERY, 0, CHUNK)
        sort_tokens(turned, 0, 2, 0, vector_copy)
        sort_tokens(turned, 0, 2, 1, scalar_copy)
        rotary = project_rotary(*units[2])
        for t in range(CHUNK, 2 * CHUNK):
            value_unit(0, t)
        store(0, VALUE, CHUNK, CHUNK)
        quantise_tokens(0, 2)

        values = [(0, t) for t in range(2 * CHUNK, TILES)] + [(1, t) for t in range(TILES)]
        beside = [0,0,0,0,1,1,1,1,1,1,1,1,1,0,1,0]
        chunks = {2: (0, 3), 9: (1, 0), 12: (1, 1), 15: (1, 2), 18: (1, 3)}
        for n, unit in enumerate(units):
            if n < 2:
                continue
            b, kind, u = unit
            rotate(rotary, *unit)
            plain_unit(*unit)
            rotary = project_rotary(*units[n + 1]) if n + 1 < len(units) else None
            if n < 16 and u % 2 == 1:
                store(b, kind, (u - 1) * UNIT, CHUNK)
            elif n >= 16 and u % 4 == 3:
                store(b, kind, (u - 3) * UNIT, HALF)
            count = beside[n] if n < len(beside) else 1
            for vb, t in values[:count]:
                value_unit(vb, t)
                if vb == 0 and t % CHUNK == CHUNK - 1:
                    store(vb, VALUE, t - CHUNK + 1, CHUNK)
                elif vb == 1 and t % HALF == HALF - 1:
                    store(vb, VALUE, t - HALF + 1, HALF)
            values = values[count:]
            if n == 4:
                turned_weights = [turn_weights(KEY, 0), turn_weights(KEY, 2)]
            if n == 5:
                sort_weights(turned_weights[0], KEY, 0, scalar_copy)
                sort_weights(turned_weights[1], KEY, 2, vector_copy)
            if n == 6:
                quantise_weights(KEY)
            if n - 1 in chunks:
                for half in range(2):
                    sort_tokens(turned, *chunks[n - 1], half, (scalar_copy if half else vector_copy))
            if n - 2 in chunks:
                quantise_tokens(*chunks[n - 2])
            if n in chunks:
                turned = turn_tokens(*chunks[n])
